import numpy as np
import ml_dtypes


def mxq(x, axis, fmt="e4m3"):
    dtype, down = {"e4m3": (ml_dtypes.float8_e4m3fn, 7), "e5m2": (ml_dtypes.float8_e5m2, 14)}[fmt]
    v = np.moveaxis(np.asarray(x, np.float32).astype(ml_dtypes.bfloat16).astype(np.float64), axis, -1)
    blocks = v.reshape(v.shape[:-1] + (-1, 32))
    amax = np.abs(blocks).max(-1, keepdims=True)
    byte = np.maximum(np.where(amax > 0, np.frexp(amax)[1] - 1 + 127, 0) - down, 1)
    scale = np.exp2(byte - 127.0)
    codes = (blocks / scale).astype(np.float32).astype(dtype).astype(np.float64)
    return np.moveaxis((codes * scale).reshape(v.shape), -1, axis)


WIDE = False


def mx_kscale(k):
    if not WIDE:
        return np.ones(k)
    levels = np.array([10, -10, 5, -5, 0])
    if k % 512:
        return np.exp2(np.random.permutation(np.resize(levels, k // 32))).repeat(32)
    a = np.empty((k // 512, 16))
    for p in range(k // 512):
        a[p, :8] = np.random.permutation(np.resize(levels, 8))
        for g in range(8):
            far = levels[np.abs(levels - a[p, g]) >= 10]
            a[p, g + 8] = far[np.random.randint(len(far))]
    return np.exp2(a.ravel()).repeat(32)


BF16 = ml_dtypes.bfloat16


def bf(x):
    return np.asarray(x, np.float32).astype(BF16)


def f64(x):
    return np.asarray(x).astype(np.float64)


B, NH, HD, H, W = 1, 3, 512, 64, 64
NEG_INF = -1e9


def draw0():
    s = mx_kscale(HD)[None, None, :, None, None]
    a = 1.3 / HD ** 0.25
    return {"q": bf(np.random.standard_normal((B, NH, HD, H, W)) * a * s),
            "k": bf(np.random.standard_normal((B, NH, HD, H, W)) * a / s)}


def core(q, k):
    qq = mxq(f64(q), 2, "e4m3")
    kq = mxq(f64(k), 2, "e4m3")
    e_h = (qq.transpose(0, 1, 4, 3, 2) @ kq.transpose(0, 1, 4, 2, 3)).transpose(0, 1, 3, 2, 4)
    e_h = np.where(np.eye(H, dtype=bool)[:, None, :], NEG_INF, e_h)
    e_w = qq.transpose(0, 1, 3, 4, 2) @ kq.transpose(0, 1, 3, 2, 4)
    e = np.concatenate([e_h, e_w], axis=-1)
    p = np.exp(e - e.max(-1, keepdims=True))
    return p / p.sum(-1, keepdims=True)


def e4m3fn_bytes(y):
    return np.clip(np.asarray(y, np.float64), -448.0, 448.0).astype(np.float32).astype(ml_dtypes.float8_e4m3fn).view(np.uint8)


def e4m3fn_values(b):
    return np.asarray(b, np.uint8).view(ml_dtypes.float8_e4m3fn).astype(np.float64)


def setup_inputs():
    d = draw0()
    x0 = np.asarray(d['q']).astype(np.float64)
    s = (np.max(np.abs(x0), axis=(0, 1, 3, 4), keepdims=True) / 448.0).astype(np.float32)
    out = {}
    for k, v in d.items():
        if k == 'q':
            out['q_bytes'] = e4m3fn_bytes(x0 / s.astype(np.float64))
            out['q_scale'] = s
        else:
            out[k] = v
    return out


def reference(q_bytes, q_scale, k):
    return core(e4m3fn_values(q_bytes) * q_scale.astype(np.float64), k)

@@ -1,0 +1,229 @@
+from contextlib import ExitStack
+
+import concourse.mybir as mybir
+from concourse.masks import make_identity
+
+NH, HD, H, W = 3, 512, 64, 64
+FLOPS = 2 * NH * H * W * (H + W) * HD
+
+F32 = mybir.dt.float32
+BF16 = mybir.dt.bfloat16
+I32 = mybir.dt.int32
+U8 = mybir.dt.uint8
+FP8 = mybir.dt.float8_e4m3fn
+FP8X4 = mybir.dt.float8_e4m3fn_x4
+ACT = mybir.ActivationFunctionType
+ALU = mybir.AluOpType
+AX = mybir.AxisListType
+
+P = 128
+PACK = 4
+ROWS = 16
+CH = ROWS * W
+NCH = H // ROWS
+PAIRS = ROWS // 2
+S = H * W
+
+
+def tile_multiheadcrisscrossattention_pa_kernel(tc, q_bytes, q_scale, k, out):
+    nc = tc.nc
+    qv = q_bytes.rearrange("b n (p t) h w -> (b n) p t (h w)", t=PACK)
+    kv = k.rearrange("b n (p t) h w -> (b n) p t (h w)", t=PACK)
+    ov = out.rearrange(
+        "a n (c hh b g) (wp ww) k -> (a n) c b (g wp) hh (ww k)", c=NCH, hh=2, b=2, g=4, ww=2
+    )
+
+    with ExitStack() as ctx:
+        const = ctx.enter_context(tc.tile_pool(name="const", bufs=1))
+        load = ctx.enter_context(tc.tile_pool(name="load", bufs=3))
+        stage = ctx.enter_context(tc.tile_pool(name="stage", bufs=3))
+        perm = ctx.enter_context(tc.tile_pool(name="perm", bufs=1))
+        energy = ctx.enter_context(tc.tile_pool(name="energy", bufs=2))
+        soft = ctx.enter_context(tc.tile_pool(name="soft", bufs=3))
+        psum_mm = ctx.enter_context(tc.psum_pool(name="psum_mm", bufs=4))
+        psum_t = ctx.enter_context(tc.psum_pool(name="psum_t", bufs=4))
+
+        warm = const.tile([P, 1], F32, name="warm")
+        nc.vector.memset(warm, 0.0)
+        warm2 = const.tile([P, 1], F32, name="warm2")
+        nc.scalar.activation(out=warm2, in_=warm, func=ACT.Exp)
+
+        qs = const.tile([P, PACK], F32, name="qs")
+        nc.sync.dma_start(out=qs, in_=q_scale.rearrange("a b (p t) c d -> p (a b t c d)", t=PACK))
+
+        ident = const.tile([P, P], F32, name="ident")
+        make_identity(nc, ident)
+        pairs_of_cols = ident.rearrange("p (m e) -> p e m", e=2)
+        maskt = const.tile([P, H, 32], F32, name="maskt")
+        nc.vector.tensor_scalar(
+            out=maskt, in0=ident[:, 0:H].unsqueeze(2).to_broadcast([P, H, 32]), scalar1=-1.0e9, scalar2=None, op0=ALU.mult
+        )
+        pick = []
+        for ww in range(2):
+            pm = const.tile([P, 2, H], F32, name="pick%d" % ww)
+            nc.vector.tensor_copy(out=pm[:, 0], in_=pairs_of_cols[:, ww])
+            nc.vector.tensor_copy(out=pm[:, 1], in_=pairs_of_cols[:, 1 - ww])
+            pick.append(pm)
+
+        planes = []
+        for i in range(3):
+            pl = const.tile([P, CH], U8, name="pl%d" % i, align_bytes=64)
+            nc.vector.memset(pl.bitcast(I32), 0)
+            planes.append(pl)
+
+        for n in range(NH):
+            qcp = perm.tile([P, S], I32, name="qcp", align_bytes=64)
+            kcp = perm.tile([P, S], I32, name="kcp", align_bytes=64)
+            sp = perm.tile([P, S], U8, name="sp", align_bytes=64)
+            xr = energy.tile([P, 2 * NCH, 2, 4, 32], F32, name="xr")
+            xc = energy.tile([P, 2, H, 32], F32, name="xc", bufs=1)
+
+            for c in range(NCH):
+                cols = slice(c * CH, (c + 1) * CH)
+                qb = load.tile([P, PACK, CH], U8, name="qb")
+                kr = load.tile([P, PACK, CH], BF16, name="kr")
+                if n == 0 and c == 0:
+                    nc.sync.dma_start(out=kr[:, :, 0 : CH // 2], in_=kv[n, :, :, 0 : CH // 2])
+                    nc.sync.dma_start(out=qb, in_=qv[n, :, :, cols])
+                    nc.sync.dma_start(out=kr[:, :, CH // 2 : CH], in_=kv[n, :, :, CH // 2 : CH])
+                else:
+                    nc.sync.dma_start(out=qb, in_=qv[n, :, :, cols])
+                    nc.sync.dma_start(out=kr, in_=kv[n, :, :, cols])
+
+                qw = stage.tile([P, PACK, CH], BF16, name="qw")
+                for t in range(PACK):
+                    nc.scalar.activation(
+                        out=qw[:, t, :], in_=qb[:, t, :].bitcast(FP8), func=ACT.Copy, scale=qs[:, t : t + 1]
+                    )
+
+                qg = stage.tile([P, CH * PACK], BF16, name="qg", align_bytes=64)
+                kg = stage.tile([P, CH * PACK], BF16, name="kg", align_bytes=64)
+                for dst, src, on_scalar in ((kg, kr, c == 2), (qg, qw, False)):
+                    dv = dst.rearrange("p (l hh c i t) -> p hh l c t i", l=PAIRS, hh=2, i=4, t=PACK)
+                    sv = src.rearrange("p t (hh l c i) -> p hh l c t i", hh=2, l=PAIRS, i=4)
+                    for hh in range(2):
+                        if on_scalar:
+                            nc.scalar.copy(out=dv[:, hh], in_=sv[:, hh])
+                        else:
+                            nc.vector.tensor_copy(out=dv[:, hh], in_=sv[:, hh])
+
+                qc = stage.tile([P, CH], I32, name="qc", align_bytes=64)
+                kc = stage.tile([P, CH], I32, name="kc", align_bytes=64)
+                pl = planes[(n * NCH + c) % 3]
+                qpl = pl
+                kpl = pl[4:P]
+                for u in range(2):
+                    nc.vector.quantize_mx(
+                        out=kc[:, u * 512 : (u + 1) * 512].bitcast(FP8X4),
+                        scales=kpl[:, u * 512 : (u + 1) * 512],
+                        in_=kg[:, u * 2048 : (u + 1) * 2048],
+                    )
+                nc.vector.quantize_mx(out=qc.bitcast(FP8X4), scales=qpl, in_=qg)
+
+                for dst, src in ((kcp, kc), (qcp, qc), (sp, pl)):
+                    nc.vector.tensor_copy(
+                        out=dst.rearrange("p (wp c hh l ww) -> p c wp hh l ww", c=NCH, hh=2, l=PAIRS, ww=2)[:, c],
+                        in_=src.rearrange("p (l hh wp ww) -> p wp hh l ww", l=PAIRS, hh=2, ww=2),
+                    )
+
+                for b in range(2):
+                    ps = psum_mm.tile([P, 512], F32, name="ps")
+                    for g in range(4):
+                        lc = slice((4 * b + g) * P, (4 * b + g + 1) * P)
+                        nc.tensor.matmul_mx(
+                            out=ps[:, g * P : (g + 1) * P],
+                            lhsT=kc[:, lc].bitcast(FP8X4),
+                            lhsT_scale=kpl[:, lc],
+                            rhs=qc[:, lc].bitcast(FP8X4),
+                            rhs_scale=qpl[:, lc],
+                            start=True,
+                            stop=True,
+                        )
+                    for x in range(2):
+                        half = slice(64 * x, 64 * x + 64)
+                        nc.scalar.copy(
+                            out=xr[half, 2 * c + b],
+                            in_=ps[half, :].rearrange("p (g y wp ww) -> p y ww g wp", g=4, y=2, ww=2)[:, x],
+                        )
+
+            for bank in range(8):
+                ps = psum_mm.tile([P, 512], F32, name="ps")
+                for g in range(4):
+                    lc = slice((4 * bank + g) * P, (4 * bank + g + 1) * P)
+                    nc.tensor.matmul_mx(
+                        out=ps[:, g * P : (g + 1) * P],
+                        lhsT=kcp[:, lc].bitcast(FP8X4),
+                        lhsT_scale=sp[4:P, lc],
+                        rhs=qcp[:, lc].bitcast(FP8X4),
+                        rhs_scale=sp[:, lc],
+                        start=True,
+                        stop=True,
+                    )
+                if n == NH - 1 and bank % 2 == 1:
+                    nc.vector.tensor_copy(
+                        out=xc[:, :, :, 4 * bank : 4 * bank + 4],
+                        in_=ps.rearrange("p (g h ww) -> p ww h g", g=4, ww=2),
+                    )
+                else:
+                    nc.scalar.copy(
+                        out=xc[:, :, :, 4 * bank : 4 * bank + 4],
+                        in_=ps.rearrange("p (g h ww) -> p ww h g", g=4, ww=2),
+                    )
+
+            for c in range(NCH):
+                for b in range(2):
+                    tp = psum_t.tile([P, 2, 2, P], F32, name="tp")
+                    for hh in range(2):
+                        h0 = ROWS * c + 8 * hh + 4 * b
+                        for ww in range(2):
+                            nc.tensor.matmul(
+                                tp[:, hh, ww, :],
+                                lhsT=xc[:, ww, h0 : h0 + 4, :].rearrange("p a b -> p (a b)"),
+                                rhs=pick[ww].rearrange("p a b -> p (a b)"),
+                                start=True,
+                                stop=False,
+                                is_transpose=True,
+                            )
+                            nc.tensor.matmul(
+                                tp[:, hh, ww, :],
+                                lhsT=maskt[:, h0 : h0 + 4, :].rearrange("p a b -> p (a b)"),
+                                rhs=ident,
+                                start=False,
+                                stop=True,
+                                is_transpose=True,
+                            )
+                    for ww in range(2):
+                        nc.tensor.transpose(
+                            tp[:, :, ww, H : 2 * H],
+                            xr[:, 2 * c + b, ww].rearrange("p a b -> p (a b)"),
+                            ident,
+                        )
+                    nmx = soft.tile([P, 4], F32, name="nmx")
+                    nc.vector.tensor_reduce(
+                        out=nmx, in_=tp.rearrange("p a b k -> p (a b) k"), axis=AX.X, op=ALU.max, negate=True
+                    )
+                    ex = soft.tile([P, 4, P], F32, name="ex")
+                    sm = soft.tile([P, 4], F32, name="sm")
+                    for i in range(4):
+                        nc.scalar.activation(
+                            out=ex[:, i, :],
+                            in_=tp[:, i // 2, i % 2, :],
+                            func=ACT.Exp,
+                            bias=nmx[:, i : i + 1],
+                            scale=1.0,
+                            accum_out=sm[:, i : i + 1],
+                        )
+                    rc = soft.tile([P, 4], F32, name="rc")
+                    nc.vector.reciprocal(out=rc, in_=sm)
+                    att = soft.tile([P, 4, P], F32, name="att")
+                    if n == NH - 1:
+                        for i in range(4):
+                            nc.vector.tensor_scalar(
+                                out=att[:, i, :], in0=ex[:, i, :], scalar1=rc[:, i : i + 1], scalar2=None, op0=ALU.mult
+                            )
+                    else:
+                        for i in range(4):
+                            nc.scalar.activation(
+                                out=att[:, i, :], in_=ex[:, i, :], func=ACT.Copy, scale=rc[:, i : i + 1]
+                            )
+                    nc.sync.dma_start(out=ov[n, c, b], in_=att.rearrange("p (hh ww) k -> p hh (ww k)", hh=2))

@@ -53,17 +53,28 @@ def tile_multiheadcrisscrossattention_pa_kernel(tc, q_bytes, q_scale, k, out):
 
         ident = const.tile([P, P], F32, name="ident")
         make_identity(nc, ident)
-        pairs_of_cols = ident.rearrange("p (m e) -> p e m", e=2)
         maskt = const.tile([P, H, 32], F32, name="maskt")
         nc.vector.tensor_scalar(
             out=maskt, in0=ident[:, 0:H].unsqueeze(2).to_broadcast([P, H, 32]), scalar1=-1.0e9, scalar2=None, op0=ALU.mult
         )
-        pick = []
+        by_x = ident.rearrange("p (a x w) -> p x a w", x=2, w=2)
+        mrow = const.tile([P, 2], F32, name="mrow")
+        nc.vector.tensor_reduce(out=mrow, in_=by_x, axis=AX.XY, op=ALU.add)
+        pickr = []
+        for x in range(2):
+            pm = const.tile([P, 2, 32, 2], F32, name="pickr%d" % x)
+            nc.vector.tensor_copy(out=pm[:, 0], in_=by_x[:, 1 - x])
+            nc.vector.tensor_copy(out=pm[:, 1], in_=by_x[:, x])
+            pickr.append(pm)
+        pickc = []
         for ww in range(2):
-            pm = const.tile([P, 2, H], F32, name="pick%d" % ww)
-            nc.vector.tensor_copy(out=pm[:, 0], in_=pairs_of_cols[:, ww])
-            nc.vector.tensor_copy(out=pm[:, 1], in_=pairs_of_cols[:, 1 - ww])
-            pick.append(pm)
+            pm = const.tile([P, 2, H], F32, name="pickc%d" % ww)
+            nc.vector.memset(pm, 0.0)
+            nc.vector.tensor_copy(
+                out=pm[:, 0].rearrange("p (c x l) -> p c x l", c=NCH, x=2),
+                in_=ident.rearrange("p (c l x w) -> p w c x l", c=NCH, x=2, w=2)[:, ww],
+            )
+            pickc.append(pm)
 
         planes = []
         for i in range(3):
@@ -75,8 +86,8 @@ def tile_multiheadcrisscrossattention_pa_kernel(tc, q_bytes, q_scale, k, out):
             qcp = perm.tile([P, S], I32, name="qcp", align_bytes=64)
             kcp = perm.tile([P, S], I32, name="kcp", align_bytes=64)
             sp = perm.tile([P, S], U8, name="sp", align_bytes=64)
-            xr = energy.tile([P, 2 * NCH, 2, 4, 32], F32, name="xr")
-            xc = energy.tile([P, 2, H, 32], F32, name="xc", bufs=1)
+            xr = energy.tile([P, 2 * NCH, 2, 2, 4, 32], F32, name="xr")
+            xc = energy.tile([P, 2, 2, 32, 32], F32, name="xc", bufs=1)
 
             for c in range(NCH):
                 cols = slice(c * CH, (c + 1) * CH)
@@ -96,11 +107,11 @@ def tile_multiheadcrisscrossattention_pa_kernel(tc, q_bytes, q_scale, k, out):
                         out=qw[:, t, :], in_=qb[:, t, :].bitcast(FP8), func=ACT.Copy, scale=qs[:, t : t + 1]
                     )
 
-                qg = stage.tile([P, CH * PACK], BF16, name="qg", align_bytes=64)
+                qg = stage.tile([P, CH * PACK], BF16, name="qg", align_bytes=64, bufs=2)
                 kg = stage.tile([P, CH * PACK], BF16, name="kg", align_bytes=64)
                 for dst, src, on_scalar in ((kg, kr, c == 2), (qg, qw, False)):
-                    dv = dst.rearrange("p (l hh c i t) -> p hh l c t i", l=PAIRS, hh=2, i=4, t=PACK)
-                    sv = src.rearrange("p t (hh l c i) -> p hh l c t i", hh=2, l=PAIRS, i=4)
+                    dv = dst.rearrange("p (m a hh w t) -> p hh m t a w", a=2, hh=2, w=2, t=PACK)
+                    sv = src.rearrange("p t (hh m a w) -> p hh m t a w", hh=2, a=2, w=2)
                     for hh in range(2):
                         if on_scalar:
                             nc.scalar.copy(out=dv[:, hh], in_=sv[:, hh])
@@ -120,11 +131,15 @@ def tile_multiheadcrisscrossattention_pa_kernel(tc, q_bytes, q_scale, k, out):
                     )
                 nc.vector.quantize_mx(out=qc.bitcast(FP8X4), scales=qpl, in_=qg)
 
-                for dst, src in ((kcp, kc), (qcp, qc), (sp, pl)):
+                for dst, src in ((kcp, kc), (qcp, qc)):
                     nc.vector.tensor_copy(
-                        out=dst.rearrange("p (wp c hh l ww) -> p c wp hh l ww", c=NCH, hh=2, l=PAIRS, ww=2)[:, c],
-                        in_=src.rearrange("p (l hh wp ww) -> p wp hh l ww", l=PAIRS, hh=2, ww=2),
+                        out=dst.rearrange("p (wp c l u) -> p c wp l u", c=NCH, l=PAIRS, u=4)[:, c],
+                        in_=src.rearrange("p (l wp u) -> p wp l u", l=PAIRS, u=4),
                     )
+                nc.vector.tensor_copy(
+                    out=sp.bitcast(I32).rearrange("p (wp c l) -> p c wp l", c=NCH, l=PAIRS)[:, c],
+                    in_=pl.bitcast(I32).rearrange("p (l wp) -> p wp l", l=PAIRS),
+                )
 
                 for b in range(2):
                     ps = psum_mm.tile([P, 512], F32, name="ps")
@@ -140,10 +155,11 @@ def tile_multiheadcrisscrossattention_pa_kernel(tc, q_bytes, q_scale, k, out):
                             stop=True,
                         )
                     for x in range(2):
-                        half = slice(64 * x, 64 * x + 64)
-                        nc.scalar.copy(
-                            out=xr[half, 2 * c + b],
-                            in_=ps[half, :].rearrange("p (g y wp ww) -> p y ww g wp", g=4, y=2, ww=2)[:, x],
+                        nc.scalar.activation(
+                            out=xr[:, 2 * c + b, x],
+                            in_=ps.rearrange("p (g wp x ww) -> p x ww g wp", g=4, x=2, ww=2)[:, x],
+                            func=ACT.Copy,
+                            scale=mrow[:, x : x + 1],
                         )
 
             for bank in range(8):
@@ -161,13 +177,13 @@ def tile_multiheadcrisscrossattention_pa_kernel(tc, q_bytes, q_scale, k, out):
                     )
                 if n == NH - 1 and bank % 2 == 1:
                     nc.vector.tensor_copy(
-                        out=xc[:, :, :, 4 * bank : 4 * bank + 4],
-                        in_=ps.rearrange("p (g h ww) -> p ww h g", g=4, ww=2),
+                        out=xc[:, :, :, :, 4 * bank : 4 * bank + 4],
+                        in_=ps.rearrange("p (g hi x ww) -> p ww x hi g", g=4, x=2, ww=2),
                     )
                 else:
                     nc.scalar.copy(
-                        out=xc[:, :, :, 4 * bank : 4 * bank + 4],
-                        in_=ps.rearrange("p (g h ww) -> p ww h g", g=4, ww=2),
+                        out=xc[:, :, :, :, 4 * bank : 4 * bank + 4],
+                        in_=ps.rearrange("p (g hi x ww) -> p ww x hi g", g=4, x=2, ww=2),
                     )
 
             for c in range(NCH):
@@ -175,11 +191,12 @@ def tile_multiheadcrisscrossattention_pa_kernel(tc, q_bytes, q_scale, k, out):
                     tp = psum_t.tile([P, 2, 2, P], F32, name="tp")
                     for hh in range(2):
                         h0 = ROWS * c + 8 * hh + 4 * b
+                        i0 = PAIRS * c + 4 * b
                         for ww in range(2):
                             nc.tensor.matmul(
                                 tp[:, hh, ww, :],
-                                lhsT=xc[:, ww, h0 : h0 + 4, :].rearrange("p a b -> p (a b)"),
-                                rhs=pick[ww].rearrange("p a b -> p (a b)"),
+                                lhsT=xc[:, ww, hh, i0 : i0 + 4, :].rearrange("p a b -> p (a b)"),
+                                rhs=pickc[ww].rearrange("p a b -> p (a b)"),
                                 start=True,
                                 stop=False,
                                 is_transpose=True,
@@ -189,15 +206,17 @@ def tile_multiheadcrisscrossattention_pa_kernel(tc, q_bytes, q_scale, k, out):
                                 lhsT=maskt[:, h0 : h0 + 4, :].rearrange("p a b -> p (a b)"),
                                 rhs=ident,
                                 start=False,
+                                stop=False,
+                                is_transpose=True,
+                            )
+                            nc.tensor.matmul(
+                                tp[:, hh, ww, :],
+                                lhsT=xr[:, 2 * c + b, hh, ww].rearrange("p a b -> p (a b)"),
+                                rhs=pickr[hh].rearrange("p a b c -> p (a b c)"),
+                                start=False,
                                 stop=True,
                                 is_transpose=True,
                             )
-                    for ww in range(2):
-                        nc.tensor.transpose(
-                            tp[:, :, ww, H : 2 * H],
-                            xr[:, 2 * c + b, ww].rearrange("p a b -> p (a b)"),
-                            ident,
-                        )
                     nmx = soft.tile([P, 4], F32, name="nmx")
                     nc.vector.tensor_reduce(
                         out=nmx, in_=tp.rearrange("p a b k -> p (a b) k"), axis=AX.X, op=ALU.max, negate=True

@@ -109,7 +109,7 @@ def tile_multiheadcrisscrossattention_pa_kernel(tc, q_bytes, q_scale, k, out):
 
                 qg = stage.tile([P, CH * PACK], BF16, name="qg", align_bytes=64, bufs=2)
                 kg = stage.tile([P, CH * PACK], BF16, name="kg", align_bytes=64)
-                for dst, src, on_scalar in ((kg, kr, c == 2), (qg, qw, False)):
+                for dst, src, on_scalar in ((kg, kr, (n * NCH + c) in (1, 3)), (qg, qw, False)):
                     dv = dst.rearrange("p (m a hh w t) -> p hh m t a w", a=2, hh=2, w=2, t=PACK)
                     sv = src.rearrange("p t (hh m a w) -> p hh m t a w", hh=2, a=2, w=2)
                     for hh in range(2):

@@ -58,22 +58,20 @@ def tile_multiheadcrisscrossattention_pa_kernel(tc, q_bytes, q_scale, k, out):
             out=maskt, in0=ident[:, 0:H].unsqueeze(2).to_broadcast([P, H, 32]), scalar1=-1.0e9, scalar2=None, op0=ALU.mult
         )
         by_x = ident.rearrange("p (a x w) -> p x a w", x=2, w=2)
-        mrow = const.tile([P, 2], F32, name="mrow")
-        nc.vector.tensor_reduce(out=mrow, in_=by_x, axis=AX.XY, op=ALU.add)
         pickr = []
         for x in range(2):
             pm = const.tile([P, 2, 32, 2], F32, name="pickr%d" % x)
-            nc.vector.tensor_copy(out=pm[:, 0], in_=by_x[:, 1 - x])
+            nc.vector.memset(pm, 0.0)
             nc.vector.tensor_copy(out=pm[:, 1], in_=by_x[:, x])
             pickr.append(pm)
+        mcol = const.tile([P, 2], F32, name="mcol")
+        nc.vector.tensor_reduce(out=mcol, in_=ident.rearrange("p (a w) -> p w a", w=2), axis=AX.X, op=ALU.add)
+        by_w = ident.rearrange("p (c l x w) -> p w c x l", c=NCH, x=2, w=2)
         pickc = []
         for ww in range(2):
             pm = const.tile([P, 2, H], F32, name="pickc%d" % ww)
-            nc.vector.memset(pm, 0.0)
-            nc.vector.tensor_copy(
-                out=pm[:, 0].rearrange("p (c x l) -> p c x l", c=NCH, x=2),
-                in_=ident.rearrange("p (c l x w) -> p w c x l", c=NCH, x=2, w=2)[:, ww],
-            )
+            nc.vector.tensor_copy(out=pm[:, 0].rearrange("p (c x l) -> p c x l", c=NCH, x=2), in_=by_w[:, ww])
+            nc.vector.tensor_copy(out=pm[:, 1].rearrange("p (c x l) -> p c x l", c=NCH, x=2), in_=by_w[:, 1 - ww])
             pickc.append(pm)
 
         planes = []
@@ -154,13 +152,10 @@ def tile_multiheadcrisscrossattention_pa_kernel(tc, q_bytes, q_scale, k, out):
                             start=True,
                             stop=True,
                         )
-                    for x in range(2):
-                        nc.scalar.activation(
-                            out=xr[:, 2 * c + b, x],
-                            in_=ps.rearrange("p (g wp x ww) -> p x ww g wp", g=4, x=2, ww=2)[:, x],
-                            func=ACT.Copy,
-                            scale=mrow[:, x : x + 1],
-                        )
+                    nc.scalar.copy(
+                        out=xr[:, 2 * c + b],
+                        in_=ps.rearrange("p (g wp x ww) -> p x ww g wp", g=4, x=2, ww=2),
+                    )
 
             for bank in range(8):
                 ps = psum_mm.tile([P, 512], F32, name="ps")
@@ -175,16 +170,13 @@ def tile_multiheadcrisscrossattention_pa_kernel(tc, q_bytes, q_scale, k, out):
                         start=True,
                         stop=True,
                     )
-                if n == NH - 1 and bank % 2 == 1:
-                    nc.vector.tensor_copy(
-                        out=xc[:, :, :, :, 4 * bank : 4 * bank + 4],
-                        in_=ps.rearrange("p (g hi x ww) -> p ww x hi g", g=4, x=2, ww=2),
-                    )
-                else:
-                    nc.scalar.copy(
-                        out=xc[:, :, :, :, 4 * bank : 4 * bank + 4],
-                        in_=ps.rearrange("p (g hi x ww) -> p ww x hi g", g=4, x=2, ww=2),
-                    )
+                for ww in range(2):
+                    dv = xc[:, ww, :, :, 4 * bank : 4 * bank + 4]
+                    sv = ps.rearrange("p (g hi x ww) -> p ww x hi g", g=4, x=2, ww=2)[:, ww]
+                    if n == NH - 1 and bank % 2 == 1:
+                        nc.vector.tensor_scalar(out=dv, in0=sv, scalar1=mcol[:, ww : ww + 1], scalar2=None, op0=ALU.mult)
+                    else:
+                        nc.scalar.activation(out=dv, in_=sv, func=ACT.Copy, scale=mcol[:, ww : ww + 1])
 
             for c in range(NCH):
                 for b in range(2):
@@ -195,8 +187,8 @@ def tile_multiheadcrisscrossattention_pa_kernel(tc, q_bytes, q_scale, k, out):
                         for ww in range(2):
                             nc.tensor.matmul(
                                 tp[:, hh, ww, :],
-                                lhsT=xc[:, ww, hh, i0 : i0 + 4, :].rearrange("p a b -> p (a b)"),
-                                rhs=pickc[ww].rearrange("p a b -> p (a b)"),
+                                lhsT=xr[:, 2 * c + b, hh, ww].rearrange("p a b -> p (a b)"),
+                                rhs=pickr[hh].rearrange("p a b c -> p (a b c)"),
                                 start=True,
                                 stop=False,
                                 is_transpose=True,
@@ -211,8 +203,8 @@ def tile_multiheadcrisscrossattention_pa_kernel(tc, q_bytes, q_scale, k, out):
                             )
                             nc.tensor.matmul(
                                 tp[:, hh, ww, :],
-                                lhsT=xr[:, 2 * c + b, hh, ww].rearrange("p a b -> p (a b)"),
-                                rhs=pickr[hh].rearrange("p a b c -> p (a b c)"),
+                                lhsT=xc[:, ww, hh, i0 : i0 + 4, :].rearrange("p a b -> p (a b)"),
+                                rhs=pickc[ww].rearrange("p a b -> p (a b)"),
                                 start=False,
                                 stop=True,
                                 is_transpose=True,

@@ -23,6 +23,7 @@ CH = ROWS * W
 NCH = H // ROWS
 PAIRS = ROWS // 2
 S = H * W
+K_ON_SCALAR = (1, 3)
 
 
 def tile_multiheadcrisscrossattention_pa_kernel(tc, q_bytes, q_scale, k, out):
@@ -80,161 +81,266 @@ def tile_multiheadcrisscrossattention_pa_kernel(tc, q_bytes, q_scale, k, out):
             nc.vector.memset(pl.bitcast(I32), 0)
             planes.append(pl)
 
-        for n in range(NH):
-            qcp = perm.tile([P, S], I32, name="qcp", align_bytes=64)
-            kcp = perm.tile([P, S], I32, name="kcp", align_bytes=64)
-            sp = perm.tile([P, S], U8, name="sp", align_bytes=64)
-            xr = energy.tile([P, 2 * NCH, 2, 2, 4, 32], F32, name="xr")
-            xc = energy.tile([P, 2, 2, 32, 32], F32, name="xc", bufs=1)
+        NCHUNK = NH * NCH
+        raw_q, raw_k, wide, grouped_k, grouped_q, codes, row_ps, per_head, grp = {}, {}, {}, {}, {}, {}, {}, {}, {}
 
-            for c in range(NCH):
-                cols = slice(c * CH, (c + 1) * CH)
-                qb = load.tile([P, PACK, CH], U8, name="qb")
-                kr = load.tile([P, PACK, CH], BF16, name="kr")
-                if n == 0 and c == 0:
-                    nc.sync.dma_start(out=kr[:, :, 0 : CH // 2], in_=kv[n, :, :, 0 : CH // 2])
-                    nc.sync.dma_start(out=qb, in_=qv[n, :, :, cols])
-                    nc.sync.dma_start(out=kr[:, :, CH // 2 : CH], in_=kv[n, :, :, CH // 2 : CH])
-                else:
-                    nc.sync.dma_start(out=qb, in_=qv[n, :, :, cols])
-                    nc.sync.dma_start(out=kr, in_=kv[n, :, :, cols])
+        def load_q(i):
+            n, c = divmod(i, NCH)
+            raw_q[i] = load.tile([P, PACK, CH], U8, name="qb")
+            nc.sync.dma_start(out=raw_q[i], in_=qv[n, :, :, c * CH : (c + 1) * CH])
 
-                qw = stage.tile([P, PACK, CH], BF16, name="qw")
-                for t in range(PACK):
-                    nc.scalar.activation(
-                        out=qw[:, t, :], in_=qb[:, t, :].bitcast(FP8), func=ACT.Copy, scale=qs[:, t : t + 1]
-                    )
+        def load_k(i, parts):
+            n, c = divmod(i, NCH)
+            if i not in raw_k:
+                raw_k[i] = load.tile([P, PACK, CH], BF16, name="kr")
+            for lo, hi in parts:
+                nc.sync.dma_start(out=raw_k[i][:, :, lo:hi], in_=kv[n, :, :, c * CH + lo : c * CH + hi])
 
-                qg = stage.tile([P, CH * PACK], BF16, name="qg", align_bytes=64, bufs=2)
-                kg = stage.tile([P, CH * PACK], BF16, name="kg", align_bytes=64)
-                for dst, src, on_scalar in ((kg, kr, (n * NCH + c) in (1, 3)), (qg, qw, False)):
-                    dv = dst.rearrange("p (m a hh w t) -> p hh m t a w", a=2, hh=2, w=2, t=PACK)
-                    sv = src.rearrange("p t (hh m a w) -> p hh m t a w", hh=2, a=2, w=2)
-                    for hh in range(2):
-                        if on_scalar:
-                            nc.scalar.copy(out=dv[:, hh], in_=sv[:, hh])
-                        else:
-                            nc.vector.tensor_copy(out=dv[:, hh], in_=sv[:, hh])
+        def widen(i, t):
+            if t == 0:
+                wide[i] = stage.tile([P, PACK, CH], BF16, name="qw")
+            nc.scalar.activation(
+                out=wide[i][:, t, :], in_=raw_q[i][:, t, :].bitcast(FP8), func=ACT.Copy, scale=qs[:, t : t + 1]
+            )
 
-                qc = stage.tile([P, CH], I32, name="qc", align_bytes=64)
-                kc = stage.tile([P, CH], I32, name="kc", align_bytes=64)
-                pl = planes[(n * NCH + c) % 3]
-                qpl = pl
-                kpl = pl[4:P]
-                for u in range(2):
-                    nc.vector.quantize_mx(
-                        out=kc[:, u * 512 : (u + 1) * 512].bitcast(FP8X4),
-                        scales=kpl[:, u * 512 : (u + 1) * 512],
-                        in_=kg[:, u * 2048 : (u + 1) * 2048],
-                    )
-                nc.vector.quantize_mx(out=qc.bitcast(FP8X4), scales=qpl, in_=qg)
+        def interleave(dst, src, hh, on_scalar):
+            dv = dst.rearrange("p (m a hh w t) -> p hh m t a w", a=2, hh=2, w=2, t=PACK)
+            sv = src.rearrange("p t (hh m a w) -> p hh m t a w", hh=2, a=2, w=2)
+            if on_scalar:
+                nc.scalar.copy(out=dv[:, hh], in_=sv[:, hh])
+            else:
+                nc.vector.tensor_copy(out=dv[:, hh], in_=sv[:, hh])
 
-                for dst, src in ((kcp, kc), (qcp, qc)):
-                    nc.vector.tensor_copy(
-                        out=dst.rearrange("p (wp c l u) -> p c wp l u", c=NCH, l=PAIRS, u=4)[:, c],
-                        in_=src.rearrange("p (l wp u) -> p wp l u", l=PAIRS, u=4),
-                    )
-                nc.vector.tensor_copy(
-                    out=sp.bitcast(I32).rearrange("p (wp c l) -> p c wp l", c=NCH, l=PAIRS)[:, c],
-                    in_=pl.bitcast(I32).rearrange("p (l wp) -> p wp l", l=PAIRS),
+        def interleave_k(i, hh, on_scalar):
+            if hh == 0:
+                grouped_k[i] = stage.tile([P, CH * PACK], BF16, name="kg", align_bytes=64)
+            interleave(grouped_k[i], raw_k[i], hh, on_scalar)
+
+        def interleave_q(i, hh):
+            if hh == 0:
+                grouped_q[i] = stage.tile([P, CH * PACK], BF16, name="qg", align_bytes=64, bufs=2)
+            interleave(grouped_q[i], wide[i], hh, False)
+
+        def quantise(i):
+            qc = stage.tile([P, CH], I32, name="qc", align_bytes=64)
+            kc = stage.tile([P, CH], I32, name="kc", align_bytes=64)
+            pl = planes[i % 3]
+            codes[i] = (kc, qc, pl)
+            for u in range(2):
+                nc.vector.quantize_mx(
+                    out=kc[:, u * 512 : (u + 1) * 512].bitcast(FP8X4),
+                    scales=pl[4:P, u * 512 : (u + 1) * 512],
+                    in_=grouped_k[i][:, u * 2048 : (u + 1) * 2048],
                 )
+            nc.vector.quantize_mx(out=qc.bitcast(FP8X4), scales=pl, in_=grouped_q[i])
 
-                for b in range(2):
-                    ps = psum_mm.tile([P, 512], F32, name="ps")
-                    for g in range(4):
-                        lc = slice((4 * b + g) * P, (4 * b + g + 1) * P)
-                        nc.tensor.matmul_mx(
-                            out=ps[:, g * P : (g + 1) * P],
-                            lhsT=kc[:, lc].bitcast(FP8X4),
-                            lhsT_scale=kpl[:, lc],
-                            rhs=qc[:, lc].bitcast(FP8X4),
-                            rhs_scale=qpl[:, lc],
-                            start=True,
-                            stop=True,
-                        )
-                    nc.scalar.copy(
-                        out=xr[:, 2 * c + b],
-                        in_=ps.rearrange("p (g wp x ww) -> p x ww g wp", g=4, x=2, ww=2),
-                    )
+        def to_columns(i):
+            n, c = divmod(i, NCH)
+            if c == 0:
+                per_head[n] = {
+                    "qcp": perm.tile([P, S], I32, name="qcp", align_bytes=64),
+                    "kcp": perm.tile([P, S], I32, name="kcp", align_bytes=64),
+                    "sp": perm.tile([P, S], U8, name="sp", align_bytes=64),
+                    "xr": energy.tile([P, 2 * NCH, 2, 2, 4, 32], F32, name="xr"),
+                }
+            kc, qc, pl = codes[i]
+            for dst, src in ((per_head[n]["kcp"], kc), (per_head[n]["qcp"], qc)):
+                nc.vector.tensor_copy(
+                    out=dst.rearrange("p (wp c l u) -> p c wp l u", c=NCH, l=PAIRS, u=4)[:, c],
+                    in_=src.rearrange("p (l wp u) -> p wp l u", l=PAIRS, u=4),
+                )
+            nc.vector.tensor_copy(
+                out=per_head[n]["sp"].bitcast(I32).rearrange("p (wp c l) -> p c wp l", c=NCH, l=PAIRS)[:, c],
+                in_=pl.bitcast(I32).rearrange("p (l wp) -> p wp l", l=PAIRS),
+            )
 
-            for bank in range(8):
+        def row_products(i):
+            kc, qc, pl = codes[i]
+            for b in range(2):
                 ps = psum_mm.tile([P, 512], F32, name="ps")
+                row_ps[(i, b)] = ps
                 for g in range(4):
-                    lc = slice((4 * bank + g) * P, (4 * bank + g + 1) * P)
+                    lc = slice((4 * b + g) * P, (4 * b + g + 1) * P)
                     nc.tensor.matmul_mx(
                         out=ps[:, g * P : (g + 1) * P],
-                        lhsT=kcp[:, lc].bitcast(FP8X4),
-                        lhsT_scale=sp[4:P, lc],
-                        rhs=qcp[:, lc].bitcast(FP8X4),
-                        rhs_scale=sp[:, lc],
+                        lhsT=kc[:, lc].bitcast(FP8X4),
+                        lhsT_scale=pl[4:P, lc],
+                        rhs=qc[:, lc].bitcast(FP8X4),
+                        rhs_scale=pl[:, lc],
                         start=True,
                         stop=True,
                     )
-                for ww in range(2):
-                    dv = xc[:, ww, :, :, 4 * bank : 4 * bank + 4]
-                    sv = ps.rearrange("p (g hi x ww) -> p ww x hi g", g=4, x=2, ww=2)[:, ww]
-                    if n == NH - 1 and bank % 2 == 1:
-                        nc.vector.tensor_scalar(out=dv, in0=sv, scalar1=mcol[:, ww : ww + 1], scalar2=None, op0=ALU.mult)
-                    else:
-                        nc.scalar.activation(out=dv, in_=sv, func=ACT.Copy, scale=mcol[:, ww : ww + 1])
 
-            for c in range(NCH):
-                for b in range(2):
-                    tp = psum_t.tile([P, 2, 2, P], F32, name="tp")
-                    for hh in range(2):
-                        h0 = ROWS * c + 8 * hh + 4 * b
-                        i0 = PAIRS * c + 4 * b
-                        for ww in range(2):
-                            nc.tensor.matmul(
-                                tp[:, hh, ww, :],
-                                lhsT=xr[:, 2 * c + b, hh, ww].rearrange("p a b -> p (a b)"),
-                                rhs=pickr[hh].rearrange("p a b c -> p (a b c)"),
-                                start=True,
-                                stop=False,
-                                is_transpose=True,
-                            )
-                            nc.tensor.matmul(
-                                tp[:, hh, ww, :],
-                                lhsT=maskt[:, h0 : h0 + 4, :].rearrange("p a b -> p (a b)"),
-                                rhs=ident,
-                                start=False,
-                                stop=False,
-                                is_transpose=True,
-                            )
-                            nc.tensor.matmul(
-                                tp[:, hh, ww, :],
-                                lhsT=xc[:, ww, hh, i0 : i0 + 4, :].rearrange("p a b -> p (a b)"),
-                                rhs=pickc[ww].rearrange("p a b -> p (a b)"),
-                                start=False,
-                                stop=True,
-                                is_transpose=True,
-                            )
-                    nmx = soft.tile([P, 4], F32, name="nmx")
-                    nc.vector.tensor_reduce(
-                        out=nmx, in_=tp.rearrange("p a b k -> p (a b) k"), axis=AX.X, op=ALU.max, negate=True
+        def empty_rows(i, b):
+            n, c = divmod(i, NCH)
+            nc.scalar.copy(
+                out=per_head[n]["xr"][:, 2 * c + b],
+                in_=row_ps[(i, b)].rearrange("p (g wp x ww) -> p x ww g wp", g=4, x=2, ww=2),
+            )
+
+        def columns(n, bank):
+            if bank == 0:
+                per_head[n]["xc"] = energy.tile([P, 2, 2, 32, 32], F32, name="xc", bufs=1)
+            xc, sp = per_head[n]["xc"], per_head[n]["sp"]
+            ps = psum_mm.tile([P, 512], F32, name="ps")
+            for g in range(4):
+                lc = slice((4 * bank + g) * P, (4 * bank + g + 1) * P)
+                nc.tensor.matmul_mx(
+                    out=ps[:, g * P : (g + 1) * P],
+                    lhsT=per_head[n]["kcp"][:, lc].bitcast(FP8X4),
+                    lhsT_scale=sp[4:P, lc],
+                    rhs=per_head[n]["qcp"][:, lc].bitcast(FP8X4),
+                    rhs_scale=sp[:, lc],
+                    start=True,
+                    stop=True,
+                )
+            for ww in range(2):
+                dv = xc[:, ww, :, :, 4 * bank : 4 * bank + 4]
+                sv = ps.rearrange("p (g hi x ww) -> p ww x hi g", g=4, x=2, ww=2)[:, ww]
+                if n == NH - 1 and bank % 2 == 1:
+                    nc.vector.tensor_scalar(out=dv, in0=sv, scalar1=mcol[:, ww : ww + 1], scalar2=None, op0=ALU.mult)
+                else:
+                    nc.scalar.activation(out=dv, in_=sv, func=ACT.Copy, scale=mcol[:, ww : ww + 1])
+
+        def transposes(n, j):
+            c, b = divmod(j, 2)
+            xr, xc = per_head[n]["xr"], per_head[n]["xc"]
+            tp = psum_t.tile([P, 2, 2, P], F32, name="tp")
+            grp[(n, j)] = {"tp": tp}
+            for hh in range(2):
+                h0 = ROWS * c + 8 * hh + 4 * b
+                i0 = PAIRS * c + 4 * b
+                for ww in range(2):
+                    nc.tensor.matmul(
+                        tp[:, hh, ww, :],
+                        lhsT=xr[:, 2 * c + b, hh, ww].rearrange("p a b -> p (a b)"),
+                        rhs=pickr[hh].rearrange("p a b c -> p (a b c)"),
+                        start=True,
+                        stop=False,
+                        is_transpose=True,
                     )
-                    ex = soft.tile([P, 4, P], F32, name="ex")
-                    sm = soft.tile([P, 4], F32, name="sm")
-                    for i in range(4):
-                        nc.scalar.activation(
-                            out=ex[:, i, :],
-                            in_=tp[:, i // 2, i % 2, :],
-                            func=ACT.Exp,
-                            bias=nmx[:, i : i + 1],
-                            scale=1.0,
-                            accum_out=sm[:, i : i + 1],
-                        )
-                    rc = soft.tile([P, 4], F32, name="rc")
-                    nc.vector.reciprocal(out=rc, in_=sm)
-                    att = soft.tile([P, 4, P], F32, name="att")
-                    if n == NH - 1:
-                        for i in range(4):
-                            nc.vector.tensor_scalar(
-                                out=att[:, i, :], in0=ex[:, i, :], scalar1=rc[:, i : i + 1], scalar2=None, op0=ALU.mult
-                            )
-                    else:
-                        for i in range(4):
-                            nc.scalar.activation(
-                                out=att[:, i, :], in_=ex[:, i, :], func=ACT.Copy, scale=rc[:, i : i + 1]
-                            )
-                    nc.sync.dma_start(out=ov[n, c, b], in_=att.rearrange("p (hh ww) k -> p hh (ww k)", hh=2))
+                    nc.tensor.matmul(
+                        tp[:, hh, ww, :],
+                        lhsT=maskt[:, h0 : h0 + 4, :].rearrange("p a b -> p (a b)"),
+                        rhs=ident,
+                        start=False,
+                        stop=False,
+                        is_transpose=True,
+                    )
+                    nc.tensor.matmul(
+                        tp[:, hh, ww, :],
+                        lhsT=xc[:, ww, hh, i0 : i0 + 4, :].rearrange("p a b -> p (a b)"),
+                        rhs=pickc[ww].rearrange("p a b -> p (a b)"),
+                        start=False,
+                        stop=True,
+                        is_transpose=True,
+                    )
+
+        def maxima(n, j):
+            nmx = soft.tile([P, 4], F32, name="nmx")
+            grp[(n, j)]["nmx"] = nmx
+            nc.vector.tensor_reduce(
+                out=nmx, in_=grp[(n, j)]["tp"].rearrange("p a b k -> p (a b) k"), axis=AX.X, op=ALU.max, negate=True
+            )
+
+        def exponentials(n, j):
+            ex = soft.tile([P, 4, P], F32, name="ex")
+            sm = soft.tile([P, 4], F32, name="sm")
+            grp[(n, j)]["ex"] = ex
+            grp[(n, j)]["sm"] = sm
+            for i in range(4):
+                nc.scalar.activation(
+                    out=ex[:, i, :],
+                    in_=grp[(n, j)]["tp"][:, i // 2, i % 2, :],
+                    func=ACT.Exp,
+                    bias=grp[(n, j)]["nmx"][:, i : i + 1],
+                    scale=1.0,
+                    accum_out=sm[:, i : i + 1],
+                )
+
+        def reciprocals(n, j):
+            rc = soft.tile([P, 4], F32, name="rc")
+            grp[(n, j)]["rc"] = rc
+            nc.vector.reciprocal(out=rc, in_=grp[(n, j)]["sm"])
+
+        def normalise(n, j):
+            c, b = divmod(j, 2)
+            ex, rc = grp[(n, j)]["ex"], grp[(n, j)]["rc"]
+            att = soft.tile([P, 4, P], F32, name="att")
+            for i in range(4):
+                if n == NH - 1:
+                    nc.vector.tensor_scalar(
+                        out=att[:, i, :], in0=ex[:, i, :], scalar1=rc[:, i : i + 1], scalar2=None, op0=ALU.mult
+                    )
+                else:
+                    nc.scalar.activation(out=att[:, i, :], in_=ex[:, i, :], func=ACT.Copy, scale=rc[:, i : i + 1])
+            nc.sync.dma_start(out=ov[n, c, b], in_=att.rearrange("p (hh ww) k -> p hh (ww k)", hh=2))
+
+        def groups_at(hs, offset):
+            found = []
+            for n in range(NH):
+                j = hs - 8 * (n + 1) - offset
+                if 0 <= j < 8:
+                    found.append((n, j))
+            return found
+
+        load_k(0, ((0, CH // 2),))
+        load_q(0)
+        load_k(0, ((CH // 2, CH),))
+        for i in (1, 2):
+            load_q(i)
+            load_k(i, ((0, CH),))
+        for t in range(PACK):
+            widen(0, t)
+
+        for hs in range(2 * NCHUNK + 12):
+            i, half = divmod(hs, 2)
+            busy = i < NCHUNK
+            k_on_scalar = i in K_ON_SCALAR
+            for n, j in groups_at(hs, 2):
+                maxima(n, j)
+            for n, j in groups_at(hs, 3):
+                exponentials(n, j)
+            if i + 1 < NCHUNK:
+                widen(i + 1, 2 * half)
+            if (i + 1) in K_ON_SCALAR and half == 1:
+                interleave_k(i + 1, 0, True)
+            if busy and half == 0:
+                if k_on_scalar:
+                    interleave_k(i, 1, True)
+                    interleave_q(i, 0)
+                else:
+                    interleave_k(i, 0, False)
+                    interleave_k(i, 1, False)
+            if busy and half == 1:
+                quantise(i)
+            for n, j in groups_at(hs, 3):
+                reciprocals(n, j)
+            if 1 <= i <= NCHUNK:
+                if (i - 1) % NCH == NCH - 1:
+                    if half == 0:
+                        empty_rows(i - 1, 0)
+                        empty_rows(i - 1, 1)
+                else:
+                    empty_rows(i - 1, half)
+            if i >= NCH and i % NCH == 0 and i // NCH <= NH:
+                for bank in range(4 * half, 4 * half + 4):
+                    columns(i // NCH - 1, bank)
+            if i + 1 < NCHUNK:
+                widen(i + 1, 2 * half + 1)
+            if busy and half == 0:
+                if k_on_scalar:
+                    interleave_q(i, 1)
+                else:
+                    interleave_q(i, 0)
+                    interleave_q(i, 1)
+            if busy and half == 1:
+                to_columns(i)
+                row_products(i)
+            for n, j in groups_at(hs, 3):
+                normalise(n, j)
+            for n, j in groups_at(hs, 1):
+                transposes(n, j)
+            if half == 0 and i + 3 < NCHUNK:
+                load_q(i + 3)
+                load_k(i + 3, ((0, CH),))

@@ -122,10 +122,10 @@ def tile_multiheadcrisscrossattention_pa_kernel(tc, q_bytes, q_scale, k, out):
             interleave(grouped_q[i], wide[i], hh, False)
 
         def quantise(i):
-            qc = stage.tile([P, CH], I32, name="qc", align_bytes=64)
-            kc = stage.tile([P, CH], I32, name="kc", align_bytes=64)
+            both = stage.tile([P, 2, CH], I32, name="both", align_bytes=64)
+            kc, qc = both[:, 0], both[:, 1]
             pl = planes[i % 3]
-            codes[i] = (kc, qc, pl)
+            codes[i] = (kc, qc, pl, both)
             for u in range(2):
                 nc.vector.quantize_mx(
                     out=kc[:, u * 512 : (u + 1) * 512].bitcast(FP8X4),
@@ -138,24 +138,22 @@ def tile_multiheadcrisscrossattention_pa_kernel(tc, q_bytes, q_scale, k, out):
             n, c = divmod(i, NCH)
             if c == 0:
                 per_head[n] = {
-                    "qcp": perm.tile([P, S], I32, name="qcp", align_bytes=64),
-                    "kcp": perm.tile([P, S], I32, name="kcp", align_bytes=64),
+                    "cp": perm.tile([P, 2, S], I32, name="cp", align_bytes=64),
                     "sp": perm.tile([P, S], U8, name="sp", align_bytes=64),
                     "xr": energy.tile([P, 2 * NCH, 2, 2, 4, 32], F32, name="xr"),
                 }
-            kc, qc, pl = codes[i]
-            for dst, src in ((per_head[n]["kcp"], kc), (per_head[n]["qcp"], qc)):
-                nc.vector.tensor_copy(
-                    out=dst.rearrange("p (wp c l u) -> p c wp l u", c=NCH, l=PAIRS, u=4)[:, c],
-                    in_=src.rearrange("p (l wp u) -> p wp l u", l=PAIRS, u=4),
-                )
+            kc, qc, pl, both = codes[i]
             nc.vector.tensor_copy(
-                out=per_head[n]["sp"].bitcast(I32).rearrange("p (wp c l) -> p c wp l", c=NCH, l=PAIRS)[:, c],
-                in_=pl.bitcast(I32).rearrange("p (l wp) -> p wp l", l=PAIRS),
+                out=per_head[n]["cp"].rearrange("p o (wp c l u) -> p c o wp l u", c=NCH, l=PAIRS, u=4)[:, c],
+                in_=both.rearrange("p o (l wp u) -> p o wp l u", l=PAIRS, u=4),
+            )
+            nc.vector.tensor_copy(
+                out=per_head[n]["sp"].bitcast(I32).rearrange("p (a w c l) -> p c a l w", w=2, c=NCH, l=PAIRS)[:, c],
+                in_=pl.bitcast(I32).rearrange("p (l a w) -> p a l w", l=PAIRS, w=2),
             )
 
         def row_products(i):
-            kc, qc, pl = codes[i]
+            kc, qc, pl, both = codes[i]
             for b in range(2):
                 ps = psum_mm.tile([P, 512], F32, name="ps")
                 row_ps[(i, b)] = ps
@@ -187,9 +185,9 @@ def tile_multiheadcrisscrossattention_pa_kernel(tc, q_bytes, q_scale, k, out):
                 lc = slice((4 * bank + g) * P, (4 * bank + g + 1) * P)
                 nc.tensor.matmul_mx(
                     out=ps[:, g * P : (g + 1) * P],
-                    lhsT=per_head[n]["kcp"][:, lc].bitcast(FP8X4),
+                    lhsT=per_head[n]["cp"][:, 0, lc].bitcast(FP8X4),
                     lhsT_scale=sp[4:P, lc],
-                    rhs=per_head[n]["qcp"][:, lc].bitcast(FP8X4),
+                    rhs=per_head[n]["cp"][:, 1, lc].bitcast(FP8X4),
                     rhs_scale=sp[:, lc],
                     start=True,
                     stop=True,

@@ -23,7 +23,7 @@ CH = ROWS * W
 NCH = H // ROWS
 PAIRS = ROWS // 2
 S = H * W
-K_ON_SCALAR = (1, 3)
+K_ON_SCALAR = (2, 3)
 
 
 def tile_multiheadcrisscrossattention_pa_kernel(tc, q_bytes, q_scale, k, out):
@@ -48,9 +48,6 @@ def tile_multiheadcrisscrossattention_pa_kernel(tc, q_bytes, q_scale, k, out):
         nc.vector.memset(warm, 0.0)
         warm2 = const.tile([P, 1], F32, name="warm2")
         nc.scalar.activation(out=warm2, in_=warm, func=ACT.Exp)
-
-        qs = const.tile([P, PACK], F32, name="qs")
-        nc.sync.dma_start(out=qs, in_=q_scale.rearrange("a b (p t) c d -> p (a b t c d)", t=PACK))
 
         ident = const.tile([P, P], F32, name="ident")
         make_identity(nc, ident)
@@ -114,7 +111,13 @@ def tile_multiheadcrisscrossattention_pa_kernel(tc, q_bytes, q_scale, k, out):
         def interleave_k(i, hh, on_scalar):
             if hh == 0:
                 grouped_k[i] = stage.tile([P, CH * PACK], BF16, name="kg", align_bytes=64)
-            interleave(grouped_k[i], raw_k[i], hh, on_scalar)
+            if i == 0 and hh == 0:
+                for v in range(2):
+                    dv = grouped_k[0].rearrange("p (v m a hh w t) -> p v hh m t a w", v=2, a=2, hh=2, w=2, t=PACK)
+                    sv = raw_k[0].rearrange("p t (hh v m a w) -> p v hh m t a w", hh=2, v=2, a=2, w=2)
+                    nc.vector.tensor_copy(out=dv[:, v, 0], in_=sv[:, v, 0])
+            else:
+                interleave(grouped_k[i], raw_k[i], hh, on_scalar)
 
         def interleave_q(i, hh):
             if hh == 0:
@@ -266,7 +269,7 @@ def tile_multiheadcrisscrossattention_pa_kernel(tc, q_bytes, q_scale, k, out):
             ex, rc = grp[(n, j)]["ex"], grp[(n, j)]["rc"]
             att = soft.tile([P, 4, P], F32, name="att")
             for i in range(4):
-                if n == NH - 1:
+                if n == NH - 1 or (n == NH - 2 and j >= 4):
                     nc.vector.tensor_scalar(
                         out=att[:, i, :], in0=ex[:, i, :], scalar1=rc[:, i : i + 1], scalar2=None, op0=ALU.mult
                     )
@@ -282,12 +285,14 @@ def tile_multiheadcrisscrossattention_pa_kernel(tc, q_bytes, q_scale, k, out):
                     found.append((n, j))
             return found
 
-        load_k(0, ((0, CH // 2),))
-        load_q(0)
+        load_k(0, ((0, CH // 4), (CH // 4, CH // 2)))
+        qs = const.tile([P, PACK], F32, name="qs")
+        nc.sync.dma_start(out=qs, in_=q_scale.rearrange("a b (p t) c d -> p (a b t c d)", t=PACK))
         load_k(0, ((CH // 2, CH),))
+        load_q(0)
         for i in (1, 2):
-            load_q(i)
             load_k(i, ((0, CH),))
+            load_q(i)
         for t in range(PACK):
             widen(0, t)
 

@@ -23,16 +23,15 @@ CH = ROWS * W
 NCH = H // ROWS
 PAIRS = ROWS // 2
 S = H * W
-K_ON_SCALAR = (2, 3)
+K_ON_SCALAR = (2,)
+K_ON_TENSOR = 3
 
 
 def tile_multiheadcrisscrossattention_pa_kernel(tc, q_bytes, q_scale, k, out):
     nc = tc.nc
     qv = q_bytes.rearrange("b n (p t) h w -> (b n) p t (h w)", t=PACK)
     kv = k.rearrange("b n (p t) h w -> (b n) p t (h w)", t=PACK)
-    ov = out.rearrange(
-        "a n (c hh b g) (wp ww) k -> (a n) c b (g wp) hh (ww k)", c=NCH, hh=2, b=2, g=4, ww=2
-    )
+    ov = out.rearrange("a n (c x l) (wp q ww) k -> (a n) q c (l wp) x (ww k)", c=NCH, x=2, q=2, ww=2)
 
     with ExitStack() as ctx:
         const = ctx.enter_context(tc.tile_pool(name="const", bufs=1))
@@ -51,9 +50,11 @@ def tile_multiheadcrisscrossattention_pa_kernel(tc, q_bytes, q_scale, k, out):
 
         ident = const.tile([P, P], F32, name="ident")
         make_identity(nc, ident)
-        maskt = const.tile([P, H, 32], F32, name="maskt")
+        ident_bf = const.tile([P, P], BF16, name="ident_bf")
+        nc.vector.tensor_copy(out=ident_bf, in_=ident)
+        maskt = const.tile([P, H, 16], F32, name="maskt")
         nc.vector.tensor_scalar(
-            out=maskt, in0=ident[:, 0:H].unsqueeze(2).to_broadcast([P, H, 32]), scalar1=-1.0e9, scalar2=None, op0=ALU.mult
+            out=maskt, in0=ident[:, 0:H].unsqueeze(2).to_broadcast([P, H, 16]), scalar1=-1.0e9, scalar2=None, op0=ALU.mult
         )
         by_x = ident.rearrange("p (a x w) -> p x a w", x=2, w=2)
         pickr = []
@@ -119,6 +120,26 @@ def tile_multiheadcrisscrossattention_pa_kernel(tc, q_bytes, q_scale, k, out):
             else:
                 interleave(grouped_k[i], raw_k[i], hh, on_scalar)
 
+        def pass_k(i):
+            kq = []
+            sv = raw_k[i].rearrange("p t (hh b f) -> p hh b t f", hh=2, b=4)
+            for b in range(4):
+                tp = psum_t.tile([P, 64, 2, 2, PACK], BF16, name="tp")
+                kq.append(tp)
+                for hh in range(2):
+                    nc.tensor.matmul(
+                        tp[:, :, hh].rearrange("p e w t -> p t e w"), lhsT=ident_bf, rhs=sv[:, hh, b], start=True, stop=True
+                    )
+            return kq
+
+        def empty_k(i, kq, b):
+            if b == 0:
+                grouped_k[i] = stage.tile([P, CH * PACK], BF16, name="kg", align_bytes=64)
+            nc.scalar.copy(
+                out=grouped_k[i][:, b * 1024 : (b + 1) * 1024],
+                in_=kq[b].rearrange("p e hh w t -> p (e hh w t)"),
+            )
+
         def interleave_q(i, hh):
             if hh == 0:
                 grouped_q[i] = stage.tile([P, CH * PACK], BF16, name="qg", align_bytes=64, bufs=2)
@@ -143,7 +164,7 @@ def tile_multiheadcrisscrossattention_pa_kernel(tc, q_bytes, q_scale, k, out):
                 per_head[n] = {
                     "cp": perm.tile([P, 2, S], I32, name="cp", align_bytes=64),
                     "sp": perm.tile([P, S], U8, name="sp", align_bytes=64),
-                    "xr": energy.tile([P, 2 * NCH, 2, 2, 4, 32], F32, name="xr"),
+                    "xr": energy.tile([P, NCH, 4, 2, PAIRS, 16], F32, name="xr"),
                 }
             kc, qc, pl, both = codes[i]
             nc.vector.tensor_copy(
@@ -175,17 +196,19 @@ def tile_multiheadcrisscrossattention_pa_kernel(tc, q_bytes, q_scale, k, out):
         def empty_rows(i, b):
             n, c = divmod(i, NCH)
             nc.scalar.copy(
-                out=per_head[n]["xr"][:, 2 * c + b],
-                in_=row_ps[(i, b)].rearrange("p (g wp x ww) -> p x ww g wp", g=4, x=2, ww=2),
+                out=per_head[n]["xr"][:, c, :, :, 4 * b : 4 * b + 4],
+                in_=row_ps[(i, b)].rearrange("p (g wp q u) -> p u q g wp", g=4, q=2, u=4),
             )
 
         def columns(n, bank):
             if bank == 0:
-                per_head[n]["xc"] = energy.tile([P, 2, 2, 32, 32], F32, name="xc", bufs=1)
+                per_head[n]["xc"] = energy.tile([P, 2, 2, 2, 32, 16], F32, name="xc", bufs=1)
             xc, sp = per_head[n]["xc"], per_head[n]["sp"]
+            q, r = divmod(bank, 4)
             ps = psum_mm.tile([P, 512], F32, name="ps")
             for g in range(4):
-                lc = slice((4 * bank + g) * P, (4 * bank + g + 1) * P)
+                wp = 2 * (4 * r + g) + q
+                lc = slice(wp * P, (wp + 1) * P)
                 nc.tensor.matmul_mx(
                     out=ps[:, g * P : (g + 1) * P],
                     lhsT=per_head[n]["cp"][:, 0, lc].bitcast(FP8X4),
@@ -196,7 +219,7 @@ def tile_multiheadcrisscrossattention_pa_kernel(tc, q_bytes, q_scale, k, out):
                     stop=True,
                 )
             for ww in range(2):
-                dv = xc[:, ww, :, :, 4 * bank : 4 * bank + 4]
+                dv = xc[:, ww, q, :, :, 4 * r : 4 * r + 4]
                 sv = ps.rearrange("p (g hi x ww) -> p ww x hi g", g=4, x=2, ww=2)[:, ww]
                 if n == NH - 1 and bank % 2 == 1:
                     nc.vector.tensor_scalar(out=dv, in0=sv, scalar1=mcol[:, ww : ww + 1], scalar2=None, op0=ALU.mult)
@@ -204,17 +227,17 @@ def tile_multiheadcrisscrossattention_pa_kernel(tc, q_bytes, q_scale, k, out):
                     nc.scalar.activation(out=dv, in_=sv, func=ACT.Copy, scale=mcol[:, ww : ww + 1])
 
         def transposes(n, j):
-            c, b = divmod(j, 2)
+            q, c = divmod(j, 4)
             xr, xc = per_head[n]["xr"], per_head[n]["xc"]
             tp = psum_t.tile([P, 2, 2, P], F32, name="tp")
             grp[(n, j)] = {"tp": tp}
             for hh in range(2):
-                h0 = ROWS * c + 8 * hh + 4 * b
-                i0 = PAIRS * c + 4 * b
+                h0 = ROWS * c + PAIRS * hh
+                i0 = PAIRS * c
                 for ww in range(2):
                     nc.tensor.matmul(
                         tp[:, hh, ww, :],
-                        lhsT=xr[:, 2 * c + b, hh, ww].rearrange("p a b -> p (a b)"),
+                        lhsT=xr[:, c, 2 * hh + ww, q].rearrange("p a b -> p (a b)"),
                         rhs=pickr[hh].rearrange("p a b c -> p (a b c)"),
                         start=True,
                         stop=False,
@@ -222,7 +245,7 @@ def tile_multiheadcrisscrossattention_pa_kernel(tc, q_bytes, q_scale, k, out):
                     )
                     nc.tensor.matmul(
                         tp[:, hh, ww, :],
-                        lhsT=maskt[:, h0 : h0 + 4, :].rearrange("p a b -> p (a b)"),
+                        lhsT=maskt[:, h0 : h0 + PAIRS, :].rearrange("p a b -> p (a b)"),
                         rhs=ident,
                         start=False,
                         stop=False,
@@ -230,7 +253,7 @@ def tile_multiheadcrisscrossattention_pa_kernel(tc, q_bytes, q_scale, k, out):
                     )
                     nc.tensor.matmul(
                         tp[:, hh, ww, :],
-                        lhsT=xc[:, ww, hh, i0 : i0 + 4, :].rearrange("p a b -> p (a b)"),
+                        lhsT=xc[:, ww, q, hh, i0 : i0 + PAIRS, :].rearrange("p a b -> p (a b)"),
                         rhs=pickc[ww].rearrange("p a b -> p (a b)"),
                         start=False,
                         stop=True,
@@ -265,7 +288,7 @@ def tile_multiheadcrisscrossattention_pa_kernel(tc, q_bytes, q_scale, k, out):
             nc.vector.reciprocal(out=rc, in_=grp[(n, j)]["sm"])
 
         def normalise(n, j):
-            c, b = divmod(j, 2)
+            q, c = divmod(j, 4)
             ex, rc = grp[(n, j)]["ex"], grp[(n, j)]["rc"]
             att = soft.tile([P, 4, P], F32, name="att")
             for i in range(4):
@@ -275,7 +298,7 @@ def tile_multiheadcrisscrossattention_pa_kernel(tc, q_bytes, q_scale, k, out):
                     )
                 else:
                     nc.scalar.activation(out=att[:, i, :], in_=ex[:, i, :], func=ACT.Copy, scale=rc[:, i : i + 1])
-            nc.sync.dma_start(out=ov[n, c, b], in_=att.rearrange("p (hh ww) k -> p hh (ww k)", hh=2))
+            nc.sync.dma_start(out=ov[n, q, c], in_=att.rearrange("p (hh ww) k -> p hh (ww k)", hh=2))
 
         def groups_at(hs, offset):
             found = []
@@ -300,6 +323,8 @@ def tile_multiheadcrisscrossattention_pa_kernel(tc, q_bytes, q_scale, k, out):
             i, half = divmod(hs, 2)
             busy = i < NCHUNK
             k_on_scalar = i in K_ON_SCALAR
+            if i + 1 == K_ON_TENSOR and half == 0:
+                kq = pass_k(K_ON_TENSOR)
             for n, j in groups_at(hs, 2):
                 maxima(n, j)
             for n, j in groups_at(hs, 3):
@@ -308,8 +333,15 @@ def tile_multiheadcrisscrossattention_pa_kernel(tc, q_bytes, q_scale, k, out):
                 widen(i + 1, 2 * half)
             if (i + 1) in K_ON_SCALAR and half == 1:
                 interleave_k(i + 1, 0, True)
+            if i + 1 == K_ON_TENSOR and half == 1:
+                empty_k(i + 1, kq, 0)
+                empty_k(i + 1, kq, 1)
             if busy and half == 0:
-                if k_on_scalar:
+                if i == K_ON_TENSOR:
+                    empty_k(i, kq, 2)
+                    empty_k(i, kq, 3)
+                    interleave_q(i, 0)
+                elif k_on_scalar:
                     interleave_k(i, 1, True)
                     interleave_q(i, 0)
                 else:
@@ -332,7 +364,7 @@ def tile_multiheadcrisscrossattention_pa_kernel(tc, q_bytes, q_scale, k, out):
             if i + 1 < NCHUNK:
                 widen(i + 1, 2 * half + 1)
             if busy and half == 0:
-                if k_on_scalar:
+                if k_on_scalar or i == K_ON_TENSOR:
                     interleave_q(i, 1)
                 else:
                     interleave_q(i, 0)

@@ -25,6 +25,7 @@ PAIRS = ROWS // 2
 S = H * W
 K_ON_SCALAR = (2,)
 K_ON_TENSOR = 3
+K_SHARED = (7,)
 
 
 def tile_multiheadcrisscrossattention_pa_kernel(tc, q_bytes, q_scale, k, out):
@@ -167,14 +168,21 @@ def tile_multiheadcrisscrossattention_pa_kernel(tc, q_bytes, q_scale, k, out):
                     "xr": energy.tile([P, NCH, 4, 2, PAIRS, 16], F32, name="xr"),
                 }
             kc, qc, pl, both = codes[i]
-            nc.vector.tensor_copy(
-                out=per_head[n]["cp"].rearrange("p o (wp c l u) -> p c o wp l u", c=NCH, l=PAIRS, u=4)[:, c],
-                in_=both.rearrange("p o (l wp u) -> p o wp l u", l=PAIRS, u=4),
-            )
+            cv = per_head[n]["cp"].rearrange("p o (wp q c l u) -> p c q o wp l u", q=2, c=NCH, l=PAIRS, u=4)[:, c]
+            sv = both.rearrange("p o (l wp q u) -> p q o wp l u", l=PAIRS, q=2, u=4)
+            if c == NCH - 1:
+                nc.vector.tensor_copy(out=cv[:, 0], in_=sv[:, 0])
+            else:
+                nc.vector.tensor_copy(
+                    out=per_head[n]["cp"].rearrange("p o (wp c l u) -> p c o wp l u", c=NCH, l=PAIRS, u=4)[:, c],
+                    in_=both.rearrange("p o (l wp u) -> p o wp l u", l=PAIRS, u=4),
+                )
             nc.vector.tensor_copy(
                 out=per_head[n]["sp"].bitcast(I32).rearrange("p (a w c l) -> p c a l w", w=2, c=NCH, l=PAIRS)[:, c],
                 in_=pl.bitcast(I32).rearrange("p (l a w) -> p a l w", l=PAIRS, w=2),
             )
+            if c == NCH - 1:
+                nc.vector.tensor_copy(out=cv[:, 1], in_=sv[:, 1])
 
         def row_products(i):
             kc, qc, pl, both = codes[i]
@@ -229,7 +237,10 @@ def tile_multiheadcrisscrossattention_pa_kernel(tc, q_bytes, q_scale, k, out):
         def transposes(n, j):
             q, c = divmod(j, 4)
             xr, xc = per_head[n]["xr"], per_head[n]["xc"]
-            tp = psum_t.tile([P, 2, 2, P], F32, name="tp")
+            if n == NH - 1 and j >= 4:
+                tp = psum_mm.tile([P, 2, 2, P], F32, name="ps")
+            else:
+                tp = psum_t.tile([P, 2, 2, P], F32, name="tp")
             grp[(n, j)] = {"tp": tp}
             for hh in range(2):
                 h0 = ROWS * c + PAIRS * hh
@@ -268,10 +279,15 @@ def tile_multiheadcrisscrossattention_pa_kernel(tc, q_bytes, q_scale, k, out):
             )
 
         def exponentials(n, j):
-            ex = soft.tile([P, 4, P], F32, name="ex")
-            sm = soft.tile([P, 4], F32, name="sm")
+            ex = soft.tile([P, 4, P], F32, name="ex", bufs=4)
+            if n == NH - 1 or j % 2 == 0:
+                sums = soft.tile([P, 8], F32, name="sums")
+            else:
+                sums = grp[(n, j - 1)]["sums"]
+            place = 4 * (j % 2) if n < NH - 1 else 0
+            sm = sums[:, place : place + 4]
             grp[(n, j)]["ex"] = ex
-            grp[(n, j)]["sm"] = sm
+            grp[(n, j)]["sums"] = sums
             for i in range(4):
                 nc.scalar.activation(
                     out=ex[:, i, :],
@@ -283,9 +299,14 @@ def tile_multiheadcrisscrossattention_pa_kernel(tc, q_bytes, q_scale, k, out):
                 )
 
         def reciprocals(n, j):
-            rc = soft.tile([P, 4], F32, name="rc")
-            grp[(n, j)]["rc"] = rc
-            nc.vector.reciprocal(out=rc, in_=grp[(n, j)]["sm"])
+            rc = soft.tile([P, 8], F32, name="rc")
+            if n == NH - 1:
+                nc.vector.reciprocal(out=rc[:, 0:4], in_=grp[(n, j)]["sums"][:, 0:4])
+                grp[(n, j)]["rc"] = rc[:, 0:4]
+            else:
+                nc.vector.reciprocal(out=rc, in_=grp[(n, j)]["sums"])
+                grp[(n, j - 1)]["rc"] = rc[:, 0:4]
+                grp[(n, j)]["rc"] = rc[:, 4:8]
 
         def normalise(n, j):
             q, c = divmod(j, 4)
@@ -298,12 +319,17 @@ def tile_multiheadcrisscrossattention_pa_kernel(tc, q_bytes, q_scale, k, out):
                     )
                 else:
                     nc.scalar.activation(out=att[:, i, :], in_=ex[:, i, :], func=ACT.Copy, scale=rc[:, i : i + 1])
-            nc.sync.dma_start(out=ov[n, q, c], in_=att.rearrange("p (hh ww) k -> p hh (ww k)", hh=2))
+            av = att.rearrange("p (hh ww) k -> p hh (ww k)", hh=2)
+            if n == NH - 1 and j == 7:
+                for hh in range(2):
+                    nc.sync.dma_start(out=ov[n, q, c, :, hh], in_=av[:, hh])
+            else:
+                nc.sync.dma_start(out=ov[n, q, c], in_=av)
 
         def groups_at(hs, offset):
             found = []
             for n in range(NH):
-                j = hs - 8 * (n + 1) - offset
+                j = hs - 8 * (n + 1) - offset + (1 if n == NH - 1 else 0)
                 if 0 <= j < 8:
                     found.append((n, j))
             return found
@@ -331,7 +357,7 @@ def tile_multiheadcrisscrossattention_pa_kernel(tc, q_bytes, q_scale, k, out):
                 exponentials(n, j)
             if i + 1 < NCHUNK:
                 widen(i + 1, 2 * half)
-            if (i + 1) in K_ON_SCALAR and half == 1:
+            if (i + 1 in K_ON_SCALAR or i + 1 in K_SHARED) and half == 1:
                 interleave_k(i + 1, 0, True)
             if i + 1 == K_ON_TENSOR and half == 1:
                 empty_k(i + 1, kq, 0)
@@ -345,12 +371,14 @@ def tile_multiheadcrisscrossattention_pa_kernel(tc, q_bytes, q_scale, k, out):
                     interleave_k(i, 1, True)
                     interleave_q(i, 0)
                 else:
-                    interleave_k(i, 0, False)
+                    if i not in K_SHARED:
+                        interleave_k(i, 0, False)
                     interleave_k(i, 1, False)
             if busy and half == 1:
                 quantise(i)
             for n, j in groups_at(hs, 3):
-                reciprocals(n, j)
+                if n == NH - 1 or j % 2 == 1:
+                    reciprocals(n, j)
             if 1 <= i <= NCHUNK:
                 if (i - 1) % NCH == NCH - 1:
                     if half == 0:
@@ -373,7 +401,11 @@ def tile_multiheadcrisscrossattention_pa_kernel(tc, q_bytes, q_scale, k, out):
                 to_columns(i)
                 row_products(i)
             for n, j in groups_at(hs, 3):
-                normalise(n, j)
+                if n == NH - 1:
+                    normalise(n, j)
+                elif j % 2 == 1:
+                    normalise(n, j - 1)
+                    normalise(n, j)
             for n, j in groups_at(hs, 1):
                 transposes(n, j)
             if half == 0 and i + 3 < NCHUNK:

from contextlib import ExitStack

import concourse.mybir as mybir
from concourse.masks import make_identity

NH, HD, H, W = 3, 512, 64, 64
FLOPS = 2 * NH * H * W * (H + W) * HD

F32 = mybir.dt.float32
BF16 = mybir.dt.bfloat16
I32 = mybir.dt.int32
U8 = mybir.dt.uint8
FP8 = mybir.dt.float8_e4m3fn
FP8X4 = mybir.dt.float8_e4m3fn_x4
ACT = mybir.ActivationFunctionType
ALU = mybir.AluOpType
AX = mybir.AxisListType

P = 128
PACK = 4
ROWS = 16
CH = ROWS * W
NCH = H // ROWS
PAIRS = ROWS // 2
S = H * W
K_ON_SCALAR = (2,)
K_ON_TENSOR = 3
K_SHARED = (7,)


def tile_multiheadcrisscrossattention_pa_kernel(tc, q_bytes, q_scale, k, out):
    nc = tc.nc
    qv = q_bytes.rearrange("b n (p t) h w -> (b n) p t (h w)", t=PACK)
    kv = k.rearrange("b n (p t) h w -> (b n) p t (h w)", t=PACK)
    ov = out.rearrange("a n (c x l) (wp q ww) k -> (a n) q c (l wp) x (ww k)", c=NCH, x=2, q=2, ww=2)

    with ExitStack() as ctx:
        const = ctx.enter_context(tc.tile_pool(name="const", bufs=1))
        load = ctx.enter_context(tc.tile_pool(name="load", bufs=3))
        stage = ctx.enter_context(tc.tile_pool(name="stage", bufs=3))
        perm = ctx.enter_context(tc.tile_pool(name="perm", bufs=1))
        energy = ctx.enter_context(tc.tile_pool(name="energy", bufs=2))
        soft = ctx.enter_context(tc.tile_pool(name="soft", bufs=3))
        psum_mm = ctx.enter_context(tc.psum_pool(name="psum_mm", bufs=4))
        psum_t = ctx.enter_context(tc.psum_pool(name="psum_t", bufs=4))

        warm = const.tile([P, 1], F32, name="warm")
        nc.vector.memset(warm, 0.0)
        warm2 = const.tile([P, 1], F32, name="warm2")
        nc.scalar.activation(out=warm2, in_=warm, func=ACT.Exp)

        ident = const.tile([P, P], F32, name="ident")
        make_identity(nc, ident)
        ident_bf = const.tile([P, P], BF16, name="ident_bf")
        nc.vector.tensor_copy(out=ident_bf, in_=ident)
        maskt = const.tile([P, H, 16], F32, name="maskt")
        nc.vector.tensor_scalar(
            out=maskt, in0=ident[:, 0:H].unsqueeze(2).to_broadcast([P, H, 16]), scalar1=-1.0e9, scalar2=None, op0=ALU.mult
        )
        by_x = ident.rearrange("p (a x w) -> p x a w", x=2, w=2)
        pickr = []
        for x in range(2):
            pm = const.tile([P, 2, 32, 2], F32, name="pickr%d" % x)
            nc.vector.memset(pm, 0.0)
            nc.vector.tensor_copy(out=pm[:, 1], in_=by_x[:, x])
            pickr.append(pm)
        mcol = const.tile([P, 2], F32, name="mcol")
        nc.vector.tensor_reduce(out=mcol, in_=ident.rearrange("p (a w) -> p w a", w=2), axis=AX.X, op=ALU.add)
        by_w = ident.rearrange("p (c l x w) -> p w c x l", c=NCH, x=2, w=2)
        pickc = []
        for ww in range(2):
            pm = const.tile([P, 2, H], F32, name="pickc%d" % ww)
            nc.vector.tensor_copy(out=pm[:, 0].rearrange("p (c x l) -> p c x l", c=NCH, x=2), in_=by_w[:, ww])
            nc.vector.tensor_copy(out=pm[:, 1].rearrange("p (c x l) -> p c x l", c=NCH, x=2), in_=by_w[:, 1 - ww])
            pickc.append(pm)

        planes = []
        for i in range(3):
            pl = const.tile([P, CH], U8, name="pl%d" % i, align_bytes=64)
            nc.vector.memset(pl.bitcast(I32), 0)
            planes.append(pl)

        NCHUNK = NH * NCH
        raw_q, raw_k, wide, grouped_k, grouped_q, codes, row_ps, per_head, grp = {}, {}, {}, {}, {}, {}, {}, {}, {}

        def load_q(i):
            n, c = divmod(i, NCH)
            raw_q[i] = load.tile([P, PACK, CH], U8, name="qb")
            nc.sync.dma_start(out=raw_q[i], in_=qv[n, :, :, c * CH : (c + 1) * CH])

        def load_k(i, parts):
            n, c = divmod(i, NCH)
            if i not in raw_k:
                raw_k[i] = load.tile([P, PACK, CH], BF16, name="kr")
            for lo, hi in parts:
                nc.sync.dma_start(out=raw_k[i][:, :, lo:hi], in_=kv[n, :, :, c * CH + lo : c * CH + hi])

        def widen(i, t):
            if t == 0:
                wide[i] = stage.tile([P, PACK, CH], BF16, name="qw")
            nc.scalar.activation(
                out=wide[i][:, t, :], in_=raw_q[i][:, t, :].bitcast(FP8), func=ACT.Copy, scale=qs[:, t : t + 1]
            )

        def interleave(dst, src, hh, on_scalar):
            dv = dst.rearrange("p (m a hh w t) -> p hh m t a w", a=2, hh=2, w=2, t=PACK)
            sv = src.rearrange("p t (hh m a w) -> p hh m t a w", hh=2, a=2, w=2)
            if on_scalar:
                nc.scalar.copy(out=dv[:, hh], in_=sv[:, hh])
            else:
                nc.vector.tensor_copy(out=dv[:, hh], in_=sv[:, hh])

        def interleave_k(i, hh, on_scalar):
            if hh == 0:
                grouped_k[i] = stage.tile([P, CH * PACK], BF16, name="kg", align_bytes=64)
            if i == 0 and hh == 0:
                for v in range(2):
                    dv = grouped_k[0].rearrange("p (v m a hh w t) -> p v hh m t a w", v=2, a=2, hh=2, w=2, t=PACK)
                    sv = raw_k[0].rearrange("p t (hh v m a w) -> p v hh m t a w", hh=2, v=2, a=2, w=2)
                    nc.vector.tensor_copy(out=dv[:, v, 0], in_=sv[:, v, 0])
            else:
                interleave(grouped_k[i], raw_k[i], hh, on_scalar)

        def pass_k(i):
            kq = []
            sv = raw_k[i].rearrange("p t (hh b f) -> p hh b t f", hh=2, b=4)
            for b in range(4):
                tp = psum_t.tile([P, 64, 2, 2, PACK], BF16, name="tp")
                kq.append(tp)
                for hh in range(2):
                    nc.tensor.matmul(
                        tp[:, :, hh].rearrange("p e w t -> p t e w"), lhsT=ident_bf, rhs=sv[:, hh, b], start=True, stop=True
                    )
            return kq

        def empty_k(i, kq, b):
            if b == 0:
                grouped_k[i] = stage.tile([P, CH * PACK], BF16, name="kg", align_bytes=64)
            nc.scalar.copy(
                out=grouped_k[i][:, b * 1024 : (b + 1) * 1024],
                in_=kq[b].rearrange("p e hh w t -> p (e hh w t)"),
            )

        def interleave_q(i, hh):
            if hh == 0:
                grouped_q[i] = stage.tile([P, CH * PACK], BF16, name="qg", align_bytes=64, bufs=2)
            interleave(grouped_q[i], wide[i], hh, False)

        def quantise(i):
            both = stage.tile([P, 2, CH], I32, name="both", align_bytes=64)
            kc, qc = both[:, 0], both[:, 1]
            pl = planes[i % 3]
            codes[i] = (kc, qc, pl, both)
            for u in range(2):
                nc.vector.quantize_mx(
                    out=kc[:, u * 512 : (u + 1) * 512].bitcast(FP8X4),
                    scales=pl[4:P, u * 512 : (u + 1) * 512],
                    in_=grouped_k[i][:, u * 2048 : (u + 1) * 2048],
                )
            nc.vector.quantize_mx(out=qc.bitcast(FP8X4), scales=pl, in_=grouped_q[i])

        def to_columns(i):
            n, c = divmod(i, NCH)
            if c == 0:
                per_head[n] = {
                    "cp": perm.tile([P, 2, S], I32, name="cp", align_bytes=64),
                    "sp": perm.tile([P, S], U8, name="sp", align_bytes=64),
                    "xr": energy.tile([P, NCH, 4, 2, PAIRS, 16], F32, name="xr"),
                }
            kc, qc, pl, both = codes[i]
            cv = per_head[n]["cp"].rearrange("p o (wp q c l u) -> p c q o wp l u", q=2, c=NCH, l=PAIRS, u=4)[:, c]
            sv = both.rearrange("p o (l wp q u) -> p q o wp l u", l=PAIRS, q=2, u=4)
            if c == NCH - 1:
                nc.vector.tensor_copy(out=cv[:, 0], in_=sv[:, 0])
            else:
                nc.vector.tensor_copy(
                    out=per_head[n]["cp"].rearrange("p o (wp c l u) -> p c o wp l u", c=NCH, l=PAIRS, u=4)[:, c],
                    in_=both.rearrange("p o (l wp u) -> p o wp l u", l=PAIRS, u=4),
                )
            nc.vector.tensor_copy(
                out=per_head[n]["sp"].bitcast(I32).rearrange("p (a w c l) -> p c a l w", w=2, c=NCH, l=PAIRS)[:, c],
                in_=pl.bitcast(I32).rearrange("p (l a w) -> p a l w", l=PAIRS, w=2),
            )
            if c == NCH - 1:
                nc.vector.tensor_copy(out=cv[:, 1], in_=sv[:, 1])

        def row_products(i):
            kc, qc, pl, both = codes[i]
            for b in range(2):
                ps = psum_mm.tile([P, 512], F32, name="ps")
                row_ps[(i, b)] = ps
                for g in range(4):
                    lc = slice((4 * b + g) * P, (4 * b + g + 1) * P)
                    nc.tensor.matmul_mx(
                        out=ps[:, g * P : (g + 1) * P],
                        lhsT=kc[:, lc].bitcast(FP8X4),
                        lhsT_scale=pl[4:P, lc],
                        rhs=qc[:, lc].bitcast(FP8X4),
                        rhs_scale=pl[:, lc],
                        start=True,
                        stop=True,
                    )

        def empty_rows(i, b):
            n, c = divmod(i, NCH)
            nc.scalar.copy(
                out=per_head[n]["xr"][:, c, :, :, 4 * b : 4 * b + 4],
                in_=row_ps[(i, b)].rearrange("p (g wp q u) -> p u q g wp", g=4, q=2, u=4),
            )

        def columns(n, bank):
            if bank == 0:
                per_head[n]["xc"] = energy.tile([P, 2, 2, 2, 32, 16], F32, name="xc", bufs=1)
            xc, sp = per_head[n]["xc"], per_head[n]["sp"]
            q, r = divmod(bank, 4)
            ps = psum_mm.tile([P, 512], F32, name="ps")
            for g in range(4):
                wp = 2 * (4 * r + g) + q
                lc = slice(wp * P, (wp + 1) * P)
                nc.tensor.matmul_mx(
                    out=ps[:, g * P : (g + 1) * P],
                    lhsT=per_head[n]["cp"][:, 0, lc].bitcast(FP8X4),
                    lhsT_scale=sp[4:P, lc],
                    rhs=per_head[n]["cp"][:, 1, lc].bitcast(FP8X4),
                    rhs_scale=sp[:, lc],
                    start=True,
                    stop=True,
                )
            for ww in range(2):
                dv = xc[:, ww, q, :, :, 4 * r : 4 * r + 4]
                sv = ps.rearrange("p (g hi x ww) -> p ww x hi g", g=4, x=2, ww=2)[:, ww]
                if n == NH - 1 and bank % 2 == 1:
                    nc.vector.tensor_scalar(out=dv, in0=sv, scalar1=mcol[:, ww : ww + 1], scalar2=None, op0=ALU.mult)
                else:
                    nc.scalar.activation(out=dv, in_=sv, func=ACT.Copy, scale=mcol[:, ww : ww + 1])

        def transposes(n, j):
            q, c = divmod(j, 4)
            xr, xc = per_head[n]["xr"], per_head[n]["xc"]
            if n == NH - 1 and j >= 4:
                tp = psum_mm.tile([P, 2, 2, P], F32, name="ps")
            else:
                tp = psum_t.tile([P, 2, 2, P], F32, name="tp")
            grp[(n, j)] = {"tp": tp}
            for hh in range(2):
                h0 = ROWS * c + PAIRS * hh
                i0 = PAIRS * c
                for ww in range(2):
                    nc.tensor.matmul(
                        tp[:, hh, ww, :],
                        lhsT=xr[:, c, 2 * hh + ww, q].rearrange("p a b -> p (a b)"),
                        rhs=pickr[hh].rearrange("p a b c -> p (a b c)"),
                        start=True,
                        stop=False,
                        is_transpose=True,
                    )
                    nc.tensor.matmul(
                        tp[:, hh, ww, :],
                        lhsT=maskt[:, h0 : h0 + PAIRS, :].rearrange("p a b -> p (a b)"),
                        rhs=ident,
                        start=False,
                        stop=False,
                        is_transpose=True,
                    )
                    nc.tensor.matmul(
                        tp[:, hh, ww, :],
                        lhsT=xc[:, ww, q, hh, i0 : i0 + PAIRS, :].rearrange("p a b -> p (a b)"),
                        rhs=pickc[ww].rearrange("p a b -> p (a b)"),
                        start=False,
                        stop=True,
                        is_transpose=True,
                    )

        def maxima(n, j):
            nmx = soft.tile([P, 4], F32, name="nmx")
            grp[(n, j)]["nmx"] = nmx
            nc.vector.tensor_reduce(
                out=nmx, in_=grp[(n, j)]["tp"].rearrange("p a b k -> p (a b) k"), axis=AX.X, op=ALU.max, negate=True
            )

        def exponentials(n, j):
            ex = soft.tile([P, 4, P], F32, name="ex", bufs=4)
            if n == NH - 1 or j % 2 == 0:
                sums = soft.tile([P, 8], F32, name="sums")
            else:
                sums = grp[(n, j - 1)]["sums"]
            place = 4 * (j % 2) if n < NH - 1 else 0
            sm = sums[:, place : place + 4]
            grp[(n, j)]["ex"] = ex
            grp[(n, j)]["sums"] = sums
            for i in range(4):
                nc.scalar.activation(
                    out=ex[:, i, :],
                    in_=grp[(n, j)]["tp"][:, i // 2, i % 2, :],
                    func=ACT.Exp,
                    bias=grp[(n, j)]["nmx"][:, i : i + 1],
                    scale=1.0,
                    accum_out=sm[:, i : i + 1],
                )

        def reciprocals(n, j):
            rc = soft.tile([P, 8], F32, name="rc")
            if n == NH - 1:
                nc.vector.reciprocal(out=rc[:, 0:4], in_=grp[(n, j)]["sums"][:, 0:4])
                grp[(n, j)]["rc"] = rc[:, 0:4]
            else:
                nc.vector.reciprocal(out=rc, in_=grp[(n, j)]["sums"])
                grp[(n, j - 1)]["rc"] = rc[:, 0:4]
                grp[(n, j)]["rc"] = rc[:, 4:8]

        def normalise(n, j):
            q, c = divmod(j, 4)
            ex, rc = grp[(n, j)]["ex"], grp[(n, j)]["rc"]
            att = soft.tile([P, 4, P], F32, name="att")
            for i in range(4):
                if n == NH - 1 or (n == NH - 2 and j >= 4):
                    nc.vector.tensor_scalar(
                        out=att[:, i, :], in0=ex[:, i, :], scalar1=rc[:, i : i + 1], scalar2=None, op0=ALU.mult
                    )
                else:
                    nc.scalar.activation(out=att[:, i, :], in_=ex[:, i, :], func=ACT.Copy, scale=rc[:, i : i + 1])
            av = att.rearrange("p (hh ww) k -> p hh (ww k)", hh=2)
            if n == NH - 1 and j == 7:
                for hh in range(2):
                    nc.sync.dma_start(out=ov[n, q, c, :, hh], in_=av[:, hh])
            else:
                nc.sync.dma_start(out=ov[n, q, c], in_=av)

        def groups_at(hs, offset):
            found = []
            for n in range(NH):
                j = hs - 8 * (n + 1) - offset + (1 if n == NH - 1 else 0)
                if 0 <= j < 8:
                    found.append((n, j))
            return found

        load_k(0, ((0, CH // 4), (CH // 4, CH // 2)))
        qs = const.tile([P, PACK], F32, name="qs")
        nc.sync.dma_start(out=qs, in_=q_scale.rearrange("a b (p t) c d -> p (a b t c d)", t=PACK))
        load_k(0, ((CH // 2, CH),))
        load_q(0)
        for i in (1, 2):
            load_k(i, ((0, CH),))
            load_q(i)
        for t in range(PACK):
            widen(0, t)

        for hs in range(2 * NCHUNK + 12):
            i, half = divmod(hs, 2)
            busy = i < NCHUNK
            k_on_scalar = i in K_ON_SCALAR
            if i + 1 == K_ON_TENSOR and half == 0:
                kq = pass_k(K_ON_TENSOR)
            for n, j in groups_at(hs, 2):
                maxima(n, j)
            for n, j in groups_at(hs, 3):
                exponentials(n, j)
            if i + 1 < NCHUNK:
                widen(i + 1, 2 * half)
            if (i + 1 in K_ON_SCALAR or i + 1 in K_SHARED) and half == 1:
                interleave_k(i + 1, 0, True)
            if i + 1 == K_ON_TENSOR and half == 1:
                empty_k(i + 1, kq, 0)
                empty_k(i + 1, kq, 1)
            if busy and half == 0:
                if i == K_ON_TENSOR:
                    empty_k(i, kq, 2)
                    empty_k(i, kq, 3)
                    interleave_q(i, 0)
                elif k_on_scalar:
                    interleave_k(i, 1, True)
                    interleave_q(i, 0)
                else:
                    if i not in K_SHARED:
                        interleave_k(i, 0, False)
                    interleave_k(i, 1, False)
            if busy and half == 1:
                quantise(i)
            for n, j in groups_at(hs, 3):
                if n == NH - 1 or j % 2 == 1:
                    reciprocals(n, j)
            if 1 <= i <= NCHUNK:
                if (i - 1) % NCH == NCH - 1:
                    if half == 0:
                        empty_rows(i - 1, 0)
                        empty_rows(i - 1, 1)
                else:
                    empty_rows(i - 1, half)
            if i >= NCH and i % NCH == 0 and i // NCH <= NH:
                for bank in range(4 * half, 4 * half + 4):
                    columns(i // NCH - 1, bank)
            if i + 1 < NCHUNK:
                widen(i + 1, 2 * half + 1)
            if busy and half == 0:
                if k_on_scalar or i == K_ON_TENSOR:
                    interleave_q(i, 1)
                else:
                    interleave_q(i, 0)
                    interleave_q(i, 1)
            if busy and half == 1:
                to_columns(i)
                row_products(i)
            for n, j in groups_at(hs, 3):
                if n == NH - 1:
                    normalise(n, j)
                elif j % 2 == 1:
                    normalise(n, j - 1)
                    normalise(n, j)
            for n, j in groups_at(hs, 1):
                transposes(n, j)
            if half == 0 and i + 3 < NCHUNK:
                load_q(i + 3)
                load_k(i + 3, ((0, CH),))
